import numpy as np
import ml_dtypes


def mxq(x, axis, fmt="e4m3"):
    dtype, down = {"e4m3": (ml_dtypes.float8_e4m3fn, 7), "e5m2": (ml_dtypes.float8_e5m2, 14)}[fmt]
    v = np.moveaxis(np.asarray(x, np.float32).astype(ml_dtypes.bfloat16).astype(np.float64), axis, -1)
    blocks = v.reshape(v.shape[:-1] + (-1, 32))
    amax = np.abs(blocks).max(-1, keepdims=True)
    byte = np.maximum(np.where(amax > 0, np.frexp(amax)[1] - 1 + 127, 0) - down, 1)
    scale = np.exp2(byte - 127.0)
    codes = (blocks / scale).astype(np.float32).astype(dtype).astype(np.float64)
    return np.moveaxis((codes * scale).reshape(v.shape), -1, axis)


WIDE = False


def mx_kscale(k):
    if not WIDE:
        return np.ones(k)
    levels = np.array([10, -10, 5, -5, 0])
    a = np.random.permutation(np.resize(levels, k // 512 * 4)).reshape(k // 512, 4)
    idx = np.arange(k)
    return np.exp2(a[idx // 512, idx % 128 // 32])


BF16 = ml_dtypes.bfloat16


def bf(x):
    return np.asarray(x, np.float32).astype(BF16)


def f64(x):
    return np.asarray(x).astype(np.float64)


E2M1 = np.array([0.0, 0.5, 1.0, 1.5, 2.0, 3.0, 4.0, 6.0, -0.0, -0.5, -1.0, -1.5, -2.0, -3.0, -4.0, -6.0])


def pack_weight(w, fmt):
    k, n = w.shape
    w = f64(bf(w)).reshape(k // 32, 32, n)
    amax = np.abs(w).max(1)
    if fmt == "e4m3":
        byte = np.frexp(amax)[1] - 1 + 127 - 7
    else:
        mant, ex = np.frexp(amax / 6.0)
        byte = np.where(mant > 0.5, ex, ex - 1) + 127
    byte = np.clip(np.where(amax > 0, byte, 1), 1, 254)
    scaled = (w * np.exp2(127.0 - byte)[:, None, :]).reshape(k, n).astype(np.float32)
    by_word = np.ascontiguousarray(scaled.reshape(k // 512, 128, 4, n).transpose(0, 1, 3, 2))
    if fmt == "e4m3":
        words = by_word.astype(ml_dtypes.float8_e4m3fn).view(np.uint8)
    else:
        c = by_word.astype(ml_dtypes.float4_e2m1fn).view(np.uint8) & 0xF
        words = c[..., 0::2] | (c[..., 1::2] << 4)
    return np.ascontiguousarray(words), np.ascontiguousarray(byte.astype(np.uint8).reshape(k // 512, 16, n))


def unpack_weight(words, scales, fmt):
    g, p, n, _ = words.shape
    if fmt == "e4m3":
        vals = np.ascontiguousarray(words).view(ml_dtypes.float8_e4m3fn).astype(np.float64)
    else:
        nib = np.empty((g, p, n, 4), np.uint8)
        nib[..., 0::2] = words & 0xF
        nib[..., 1::2] = words >> 4
        vals = E2M1[nib]
    vals = vals * np.repeat(np.exp2(scales.astype(np.float64) - 127.0), 8, axis=1)[..., None]
    return vals.transpose(0, 1, 3, 2).reshape(g * 512, n)


B, S, H, O, W = 8, 32, 3072, 6144, 8


def setup_inputs():
    s = mx_kscale(H)
    hidden_states = bf(np.random.standard_normal((B, S, H)) * s)
    gate_proj = np.random.standard_normal((O, H)) / np.sqrt(H) / s[None, :]
    words, scales = pack_weight(np.ascontiguousarray(gate_proj.T), "e4m3")
    return {"hidden_states": hidden_states,
            "gate_proj_words": words,
            "gate_proj_scales": scales,
            "world_size": W}


def reference(hidden_states, gate_proj_words, gate_proj_scales, world_size):
    wt = unpack_weight(gate_proj_words, gate_proj_scales, "e4m3")
    h = wt.shape[0]
    view = f64(hidden_states).reshape(-1, h)
    mm = mxq(view, 1, "e4m3") @ wt
    n, o = mm.shape
    out = mm.reshape(world_size, n // world_size, o).sum(axis=0)
    return out

@@ -1,0 +1,156 @@
+from contextlib import ExitStack
+
+import concourse.mybir as mybir
+from concourse.masks import make_identity
+
+FP8X4 = mybir.dt.float8_e4m3fn_x4
+F32 = mybir.dt.float32
+BF16 = mybir.dt.bfloat16
+U32 = mybir.dt.uint32
+U8 = mybir.dt.uint8
+I32 = mybir.dt.int32
+
+P = 128
+ROWS = 256
+H = 3072
+O = 6144
+G = H // 512
+NT = O // P
+RT = 6
+RANGES = NT // RT
+RW = RT * P
+HALF = O // 2
+BLK = 12
+FLOPS = 2 * ROWS * H * O
+
+
+def tile_testmmrsmodel_w_kernel(tc, hidden_states, gate_proj_words, gate_proj_scales, world_size, out):
+    nc = tc.nc
+    assert world_size == 8
+    J = ROWS // world_size
+    x_view = hidden_states.flatten_outer_dims()
+
+    with ExitStack() as ctx:
+        keep = ctx.enter_context(tc.tile_pool(name="keep", bufs=1))
+        wpool = ctx.enter_context(tc.tile_pool(name="wpool", bufs=1))
+        opool = ctx.enter_context(tc.tile_pool(name="opool", bufs=2))
+        psum = ctx.enter_context(tc.psum_pool(name="psum", bufs=8))
+
+        planes = keep.tile([P, 3, HALF], U8, align_bytes=64)
+        nc.vector.memset(planes[:].bitcast(I32), 0)
+        ident = keep.tile([P, P], F32)
+        make_identity(nc, ident[:])
+
+        x_sb = []
+        for m in range(2):
+            xm = keep.tile([P, H], BF16, name="x%d" % m)
+            x_sb.append(xm)
+        for ch in range(2):
+            for m in range(2):
+                cs = slice(ch * (H // 2), (ch + 1) * (H // 2))
+                nc.sync.dma_start(out=x_sb[m][:, cs], in_=x_view[m * P:(m + 1) * P, cs])
+
+        def load_scales(h):
+            runs = {}
+            for g in range(G):
+                pl = G * h + g
+                runs[pl // 4] = runs.get(pl // 4, []) + [g]
+            for s in sorted(runs):
+                gs = runs[s]
+                k0 = 4 * ((G * h + gs[0]) % 4)
+                for q in range(4):
+                    nc.sync.dma_start(
+                        out=planes[32 * q + k0:32 * q + k0 + 4 * len(gs), s, :].bitcast(I32),
+                        in_=gate_proj_scales[gs[0]:gs[0] + len(gs), 4 * q:4 * q + 4, h * HALF:(h + 1) * HALF].bitcast(I32),
+                    )
+
+        w_tiles = {}
+
+        def load_range(i):
+            for g in range(G):
+                wt = wpool.tile([P, RW], U32, name="w%d_%d" % (i, g), align_bytes=64)
+                src = gate_proj_words[g].rearrange("p n t -> p (n t)")[:, 4 * i * RW:4 * (i + 1) * RW]
+                nc.sync.dma_start(out=wt[:].bitcast(I32), in_=src.bitcast(I32))
+                w_tiles[(i, g)] = wt
+
+        load_scales(0)
+        for i in range(RANGES):
+            if i == 3:
+                load_scales(1)
+            load_range(i)
+
+        grouped = keep.tile([P, G, 4 * ROWS], BF16, align_bytes=64)
+        x_codes = keep.tile([P, G, ROWS], U32, align_bytes=64)
+        x_plane = keep.tile([P, G, ROWS], U8, align_bytes=64)
+        for g in range(G):
+            xt = psum.tile([P, 2, ROWS], F32, tag="bank")
+            for u in range(2):
+                for m in range(2):
+                    nc.tensor.transpose(
+                        xt[:, u, m * P:(m + 1) * P],
+                        x_sb[m][:].bitcast(F32)[:, 256 * g + u:256 * (g + 1):2],
+                        ident[:],
+                    )
+            dst = grouped[:, g, :].bitcast(F32).rearrange("p (r u) -> p r u", u=2)
+            if g % 2 == 0:
+                nc.vector.tensor_copy(out=dst, in_=xt[:].rearrange("p u r -> p r u"))
+            else:
+                nc.scalar.copy(out=dst, in_=xt[:].rearrange("p u r -> p r u"))
+        for g in range(G):
+            nc.vector.quantize_mx(
+                out=x_codes[:, g, :].bitcast(FP8X4),
+                scales=x_plane[:, g, :],
+                in_=grouped[:, g, :],
+            )
+
+        o_t = {}
+
+        def emit_block(b, queue):
+            tp = psum.tile([P, 512], F32, tag="bank")
+            for c in range(3):
+                nc.tensor.transpose(tp[:, c * P:(c + 1) * P], o_t[b][:, c, :], ident[:])
+            osb = opool.tile([P, 3 * P], F32)
+            nc.scalar.copy(out=osb[:], in_=tp[:, 0:3 * P])
+            for t4 in range(4):
+                c0 = b * BLK * P + t4 * 3 * P
+                queue.dma_start(out=out[:, c0:c0 + 3 * P], in_=osb[J * t4:J * (t4 + 1), :])
+
+        for i in range(RANGES):
+            accs = []
+            for t in range(RT):
+                acc = psum.tile([P, 512], F32, tag="bank")
+                accs.append(acc)
+            for g in range(G):
+                for t in range(RT):
+                    n0 = i * RW + t * P
+                    h = n0 // HALF
+                    pl = G * h + g
+                    k = 4 * (pl % 4)
+                    col = n0 - h * HALF
+                    nc.tensor.matmul_mx(
+                        out=accs[t][:, 0:ROWS],
+                        lhsT=w_tiles[(i, g)][:, t * P:(t + 1) * P].bitcast(FP8X4),
+                        lhsT_scale=planes[k:P, pl // 4, col:col + P],
+                        rhs=x_codes[:, g, :].bitcast(FP8X4),
+                        rhs_scale=x_plane[:, g, :],
+                        start=(g == 0),
+                        stop=(g == G - 1),
+                    )
+                if g == 1 and i >= 2 and i % 2 == 0:
+                    emit_block(i // 2 - 1, nc.scalar)
+            for t in range(RT):
+                tau = i * RT + t
+                b = tau // BLK
+                loc = tau % BLK
+                if loc == 0:
+                    ot = opool.tile([P, 3, P], F32)
+                    o_t[b] = ot
+                t4 = loc // 3
+                c = loc % 3
+                nc.vector.tensor_reduce(
+                    out=o_t[b][:, c, J * t4:J * (t4 + 1)],
+                    in_=accs[t][:, 0:ROWS].rearrange("p (r j) -> p j r", r=world_size),
+                    axis=mybir.AxisListType.X,
+                    op=mybir.AluOpType.add,
+                )
+        emit_block(NT // BLK - 1, nc.sync)

@@ -19,7 +19,7 @@ NT = O // P
 RT = 6
 RANGES = NT // RT
 RW = RT * P
-HALF = O // 2
+QW = 2 * RW
 BLK = 12
 FLOPS = 2 * ROWS * H * O
 
@@ -33,57 +33,76 @@ def tile_testmmrsmodel_w_kernel(tc, hidden_states, gate_proj_words, gate_proj_sc
     with ExitStack() as ctx:
         keep = ctx.enter_context(tc.tile_pool(name="keep", bufs=1))
         wpool = ctx.enter_context(tc.tile_pool(name="wpool", bufs=1))
+        stg = ctx.enter_context(tc.tile_pool(name="stg", bufs=2))
+        evp = ctx.enter_context(tc.tile_pool(name="evp", bufs=6))
         opool = ctx.enter_context(tc.tile_pool(name="opool", bufs=2))
-        psum = ctx.enter_context(tc.psum_pool(name="psum", bufs=8))
+        psum = ctx.enter_context(tc.psum_pool(name="psum", bufs=1))
+        ctx.enter_context(tc.manual_schedule())
+        ring = [0]
 
-        planes = keep.tile([P, 3, HALF], U8, align_bytes=64)
+        def bank(shape):
+            b = psum.tile(shape, F32, tag="bank%d" % (ring[0] % 8), name="bk%d" % ring[0])
+            ring[0] += 1
+            return b
+
+        planes = keep.tile([P, 2, O], U8, align_bytes=64)
         nc.vector.memset(planes[:].bitcast(I32), 0)
         ident = keep.tile([P, P], F32)
         make_identity(nc, ident[:])
+
+        SLOT = ((0, 4), (4, 2))
+        st_tiles = {}
+
+        def stage(c, slot, queue, view):
+            g0, cnt = SLOT[slot]
+            for q in range(4):
+                queue.dma_start(
+                    out=st_tiles[c][32 * q:32 * q + 4 * cnt, q, slot, :].bitcast(view),
+                    in_=gate_proj_scales[g0:g0 + cnt, 4 * q:4 * q + 4, c * QW:(c + 1) * QW].bitcast(view),
+                )
+
+        def move(c, slot):
+            cnt = SLOT[slot][1]
+            for q in range(4):
+                nc.vector.tensor_copy(
+                    out=planes[32 * q:32 * q + 4 * cnt, slot, c * QW:(c + 1) * QW].bitcast(I32),
+                    in_=st_tiles[c][32 * q:32 * q + 4 * cnt, q, slot, :].bitcast(I32),
+                )
+
+        def new_stage(c):
+            st = stg.tile([P, 4, 2, QW], U8, name="st%d" % c, tag="st", align_bytes=64)
+            st_tiles[c] = st
 
         x_sb = []
         for m in range(2):
             xm = keep.tile([P, H], BF16, name="x%d" % m)
             x_sb.append(xm)
+
+        new_stage(0)
+        stage(0, 0, nc.sync, I32)
         for ch in range(2):
             for m in range(2):
                 cs = slice(ch * (H // 2), (ch + 1) * (H // 2))
                 nc.sync.dma_start(out=x_sb[m][:, cs], in_=x_view[m * P:(m + 1) * P, cs])
-
-        def load_scales(h):
-            runs = {}
-            for g in range(G):
-                pl = G * h + g
-                runs[pl // 4] = runs.get(pl // 4, []) + [g]
-            for s in sorted(runs):
-                gs = runs[s]
-                k0 = 4 * ((G * h + gs[0]) % 4)
-                for q in range(4):
-                    nc.sync.dma_start(
-                        out=planes[32 * q + k0:32 * q + k0 + 4 * len(gs), s, :].bitcast(I32),
-                        in_=gate_proj_scales[gs[0]:gs[0] + len(gs), 4 * q:4 * q + 4, h * HALF:(h + 1) * HALF].bitcast(I32),
-                    )
+        stage(0, 1, nc.sync, I32)
+        new_stage(1)
+        stage(1, 0, nc.gpsimd, F32)
+        stage(1, 1, nc.gpsimd, F32)
 
         w_tiles = {}
-
-        def load_range(i):
+        for i in range(RANGES):
             for g in range(G):
                 wt = wpool.tile([P, RW], U32, name="w%d_%d" % (i, g), align_bytes=64)
                 src = gate_proj_words[g].rearrange("p n t -> p (n t)")[:, 4 * i * RW:4 * (i + 1) * RW]
                 nc.sync.dma_start(out=wt[:].bitcast(I32), in_=src.bitcast(I32))
                 w_tiles[(i, g)] = wt
 
-        load_scales(0)
-        for i in range(RANGES):
-            if i == 3:
-                load_scales(1)
-            load_range(i)
-
         grouped = keep.tile([P, G, 4 * ROWS], BF16, align_bytes=64)
         x_codes = keep.tile([P, G, ROWS], U32, align_bytes=64)
         x_plane = keep.tile([P, G, ROWS], U8, align_bytes=64)
-        for g in range(G):
-            xt = psum.tile([P, 2, ROWS], F32, tag="bank")
+
+        def flip(g):
+            xt = bank([P, 2, ROWS])
             for u in range(2):
                 for m in range(2):
                     nc.tensor.transpose(
@@ -92,21 +111,31 @@ def tile_testmmrsmodel_w_kernel(tc, hidden_states, gate_proj_words, gate_proj_sc
                         ident[:],
                     )
             dst = grouped[:, g, :].bitcast(F32).rearrange("p (r u) -> p r u", u=2)
-            if g % 2 == 0:
-                nc.vector.tensor_copy(out=dst, in_=xt[:].rearrange("p u r -> p r u"))
-            else:
-                nc.scalar.copy(out=dst, in_=xt[:].rearrange("p u r -> p r u"))
-        for g in range(G):
+            nc.scalar.copy(out=dst, in_=xt[:].rearrange("p u r -> p r u"))
+
+        def quantise(g):
             nc.vector.quantize_mx(
                 out=x_codes[:, g, :].bitcast(FP8X4),
                 scales=x_plane[:, g, :],
                 in_=grouped[:, g, :],
             )
 
+        move(0, 0)
+        for g in range(G):
+            flip(g)
+        for g in range(3):
+            quantise(g)
+        move(0, 1)
+        for g in range(3, G):
+            quantise(g)
+        new_stage(2)
+        stage(2, 0, nc.gpsimd, F32)
+        stage(2, 1, nc.gpsimd, F32)
+
         o_t = {}
 
         def emit_block(b, queue):
-            tp = psum.tile([P, 512], F32, tag="bank")
+            tp = bank([P, 512])
             for c in range(3):
                 nc.tensor.transpose(tp[:, c * P:(c + 1) * P], o_t[b][:, c, :], ident[:])
             osb = opool.tile([P, 3 * P], F32)
@@ -115,22 +144,29 @@ def tile_testmmrsmodel_w_kernel(tc, hidden_states, gate_proj_words, gate_proj_sc
                 c0 = b * BLK * P + t4 * 3 * P
                 queue.dma_start(out=out[:, c0:c0 + 3 * P], in_=osb[J * t4:J * (t4 + 1), :])
 
+        def reduce_tile(tau, src):
+            b = tau // BLK
+            loc = tau % BLK
+            nc.vector.tensor_reduce(
+                out=o_t[b][:, loc % 3, J * (loc // 3):J * (loc // 3 + 1)],
+                in_=src.rearrange("p (r j) -> p j r", r=world_size),
+                axis=mybir.AxisListType.X,
+                op=mybir.AluOpType.add,
+            )
+
+        MOVES = {0: ((1, 0), (1, 1)), 1: ((2, 0),), 2: ((2, 1),), 3: ((3, 0),), 4: ((3, 1),)}
+
         for i in range(RANGES):
             accs = []
             for t in range(RT):
-                acc = psum.tile([P, 512], F32, tag="bank")
-                accs.append(acc)
+                accs.append(bank([P, 512]))
             for g in range(G):
                 for t in range(RT):
                     n0 = i * RW + t * P
-                    h = n0 // HALF
-                    pl = G * h + g
-                    k = 4 * (pl % 4)
-                    col = n0 - h * HALF
                     nc.tensor.matmul_mx(
                         out=accs[t][:, 0:ROWS],
                         lhsT=w_tiles[(i, g)][:, t * P:(t + 1) * P].bitcast(FP8X4),
-                        lhsT_scale=planes[k:P, pl // 4, col:col + P],
+                        lhsT_scale=planes[4 * (g % 4):P, g // 4, n0:n0 + P],
                         rhs=x_codes[:, g, :].bitcast(FP8X4),
                         rhs_scale=x_plane[:, g, :],
                         start=(g == 0),
@@ -138,19 +174,22 @@ def tile_testmmrsmodel_w_kernel(tc, hidden_states, gate_proj_words, gate_proj_sc
                     )
                 if g == 1 and i >= 2 and i % 2 == 0:
                     emit_block(i // 2 - 1, nc.scalar)
-            for t in range(RT):
-                tau = i * RT + t
-                b = tau // BLK
-                loc = tau % BLK
-                if loc == 0:
-                    ot = opool.tile([P, 3, P], F32)
-                    o_t[b] = ot
-                t4 = loc // 3
-                c = loc % 3
-                nc.vector.tensor_reduce(
-                    out=o_t[b][:, c, J * t4:J * (t4 + 1)],
-                    in_=accs[t][:, 0:ROWS].rearrange("p (r j) -> p j r", r=world_size),
-                    axis=mybir.AxisListType.X,
-                    op=mybir.AluOpType.add,
-                )
+            if i % 2 == 0:
+                ot = opool.tile([P, 3, P], F32)
+                o_t[i // 2] = ot
+            evs = {}
+            for t in range(1, RT, 2):
+                ev = evp.tile([P, ROWS], F32)
+                nc.scalar.copy(out=ev[:], in_=accs[t][:, 0:ROWS])
+                evs[t] = ev
+            for t in range(0, RT, 2):
+                reduce_tile(i * RT + t, accs[t][:, 0:ROWS])
+            for t in range(1, RT, 2):
+                reduce_tile(i * RT + t, evs[t][:])
+            for c, slot in MOVES.get(i, ()):
+                move(c, slot)
+            if i == 0:
+                new_stage(3)
+                stage(3, 0, nc.gpsimd, F32)
+                stage(3, 1, nc.gpsimd, F32)
         emit_block(NT // BLK - 1, nc.sync)

@@ -35,7 +35,7 @@ def tile_testmmrsmodel_w_kernel(tc, hidden_states, gate_proj_words, gate_proj_sc
         wpool = ctx.enter_context(tc.tile_pool(name="wpool", bufs=1))
         stg = ctx.enter_context(tc.tile_pool(name="stg", bufs=2))
         evp = ctx.enter_context(tc.tile_pool(name="evp", bufs=6))
-        opool = ctx.enter_context(tc.tile_pool(name="opool", bufs=2))
+        opool = ctx.enter_context(tc.tile_pool(name="opool", bufs=4))
         psum = ctx.enter_context(tc.psum_pool(name="psum", bufs=1))
         ctx.enter_context(tc.manual_schedule())
         ring = [0]
@@ -111,7 +111,10 @@ def tile_testmmrsmodel_w_kernel(tc, hidden_states, gate_proj_words, gate_proj_sc
                         ident[:],
                     )
             dst = grouped[:, g, :].bitcast(F32).rearrange("p (r u) -> p r u", u=2)
-            nc.scalar.copy(out=dst, in_=xt[:].rearrange("p u r -> p r u"))
+            nc.scalar.copy(
+                out=dst.rearrange("p (j r) u -> p j r u", r=world_size),
+                in_=xt[:].rearrange("p u (r j) -> p j r u", r=world_size),
+            )
 
         def quantise(g):
             nc.vector.quantize_mx(
@@ -149,7 +152,7 @@ def tile_testmmrsmodel_w_kernel(tc, hidden_states, gate_proj_words, gate_proj_sc
             loc = tau % BLK
             nc.vector.tensor_reduce(
                 out=o_t[b][:, loc % 3, J * (loc // 3):J * (loc // 3 + 1)],
-                in_=src.rearrange("p (r j) -> p j r", r=world_size),
+                in_=src.rearrange("p (j r) -> p j r", r=world_size),
                 axis=mybir.AxisListType.X,
                 op=mybir.AluOpType.add,
             )
@@ -173,7 +176,7 @@ def tile_testmmrsmodel_w_kernel(tc, hidden_states, gate_proj_words, gate_proj_sc
                         stop=(g == G - 1),
                     )
                 if g == 1 and i >= 2 and i % 2 == 0:
-                    emit_block(i // 2 - 1, nc.scalar)
+                    emit_block(i // 2 - 1, nc.gpsimd)
             if i % 2 == 0:
                 ot = opool.tile([P, 3, P], F32)
                 o_t[i // 2] = ot

from contextlib import ExitStack

import concourse.mybir as mybir
from concourse.masks import make_identity

FP8X4 = mybir.dt.float8_e4m3fn_x4
F32 = mybir.dt.float32
BF16 = mybir.dt.bfloat16
U32 = mybir.dt.uint32
U8 = mybir.dt.uint8
I32 = mybir.dt.int32

P = 128
ROWS = 256
H = 3072
O = 6144
G = H // 512
NT = O // P
RT = 6
RANGES = NT // RT
RW = RT * P
QW = 2 * RW
BLK = 12
FLOPS = 2 * ROWS * H * O


def tile_testmmrsmodel_w_kernel(tc, hidden_states, gate_proj_words, gate_proj_scales, world_size, out):
    nc = tc.nc
    assert world_size == 8
    J = ROWS // world_size
    x_view = hidden_states.flatten_outer_dims()

    with ExitStack() as ctx:
        keep = ctx.enter_context(tc.tile_pool(name="keep", bufs=1))
        wpool = ctx.enter_context(tc.tile_pool(name="wpool", bufs=1))
        stg = ctx.enter_context(tc.tile_pool(name="stg", bufs=2))
        evp = ctx.enter_context(tc.tile_pool(name="evp", bufs=6))
        opool = ctx.enter_context(tc.tile_pool(name="opool", bufs=4))
        psum = ctx.enter_context(tc.psum_pool(name="psum", bufs=1))
        ctx.enter_context(tc.manual_schedule())
        ring = [0]

        def bank(shape):
            b = psum.tile(shape, F32, tag="bank%d" % (ring[0] % 8), name="bk%d" % ring[0])
            ring[0] += 1
            return b

        planes = keep.tile([P, 2, O], U8, align_bytes=64)
        nc.vector.memset(planes[:].bitcast(I32), 0)
        ident = keep.tile([P, P], F32)
        make_identity(nc, ident[:])

        SLOT = ((0, 4), (4, 2))
        st_tiles = {}

        def stage(c, slot, queue, view):
            g0, cnt = SLOT[slot]
            for q in range(4):
                queue.dma_start(
                    out=st_tiles[c][32 * q:32 * q + 4 * cnt, q, slot, :].bitcast(view),
                    in_=gate_proj_scales[g0:g0 + cnt, 4 * q:4 * q + 4, c * QW:(c + 1) * QW].bitcast(view),
                )

        def move(c, slot):
            cnt = SLOT[slot][1]
            for q in range(4):
                nc.vector.tensor_copy(
                    out=planes[32 * q:32 * q + 4 * cnt, slot, c * QW:(c + 1) * QW].bitcast(I32),
                    in_=st_tiles[c][32 * q:32 * q + 4 * cnt, q, slot, :].bitcast(I32),
                )

        def new_stage(c):
            st = stg.tile([P, 4, 2, QW], U8, name="st%d" % c, tag="st", align_bytes=64)
            st_tiles[c] = st

        x_sb = []
        for m in range(2):
            xm = keep.tile([P, H], BF16, name="x%d" % m)
            x_sb.append(xm)

        new_stage(0)
        stage(0, 0, nc.sync, I32)
        for ch in range(2):
            for m in range(2):
                cs = slice(ch * (H // 2), (ch + 1) * (H // 2))
                nc.sync.dma_start(out=x_sb[m][:, cs], in_=x_view[m * P:(m + 1) * P, cs])
        stage(0, 1, nc.sync, I32)
        new_stage(1)
        stage(1, 0, nc.gpsimd, F32)
        stage(1, 1, nc.gpsimd, F32)

        w_tiles = {}
        for i in range(RANGES):
            for g in range(G):
                wt = wpool.tile([P, RW], U32, name="w%d_%d" % (i, g), align_bytes=64)
                src = gate_proj_words[g].rearrange("p n t -> p (n t)")[:, 4 * i * RW:4 * (i + 1) * RW]
                nc.sync.dma_start(out=wt[:].bitcast(I32), in_=src.bitcast(I32))
                w_tiles[(i, g)] = wt

        grouped = keep.tile([P, G, 4 * ROWS], BF16, align_bytes=64)
        x_codes = keep.tile([P, G, ROWS], U32, align_bytes=64)
        x_plane = keep.tile([P, G, ROWS], U8, align_bytes=64)

        def flip(g):
            xt = bank([P, 2, ROWS])
            for u in range(2):
                for m in range(2):
                    nc.tensor.transpose(
                        xt[:, u, m * P:(m + 1) * P],
                        x_sb[m][:].bitcast(F32)[:, 256 * g + u:256 * (g + 1):2],
                        ident[:],
                    )
            dst = grouped[:, g, :].bitcast(F32).rearrange("p (r u) -> p r u", u=2)
            nc.scalar.copy(
                out=dst.rearrange("p (j r) u -> p j r u", r=world_size),
                in_=xt[:].rearrange("p u (r j) -> p j r u", r=world_size),
            )

        def quantise(g):
            nc.vector.quantize_mx(
                out=x_codes[:, g, :].bitcast(FP8X4),
                scales=x_plane[:, g, :],
                in_=grouped[:, g, :],
            )

        move(0, 0)
        for g in range(G):
            flip(g)
        for g in range(3):
            quantise(g)
        move(0, 1)
        for g in range(3, G):
            quantise(g)
        new_stage(2)
        stage(2, 0, nc.gpsimd, F32)
        stage(2, 1, nc.gpsimd, F32)

        o_t = {}

        def emit_block(b, queue):
            tp = bank([P, 512])
            for c in range(3):
                nc.tensor.transpose(tp[:, c * P:(c + 1) * P], o_t[b][:, c, :], ident[:])
            osb = opool.tile([P, 3 * P], F32)
            nc.scalar.copy(out=osb[:], in_=tp[:, 0:3 * P])
            for t4 in range(4):
                c0 = b * BLK * P + t4 * 3 * P
                queue.dma_start(out=out[:, c0:c0 + 3 * P], in_=osb[J * t4:J * (t4 + 1), :])

        def reduce_tile(tau, src):
            b = tau // BLK
            loc = tau % BLK
            nc.vector.tensor_reduce(
                out=o_t[b][:, loc % 3, J * (loc // 3):J * (loc // 3 + 1)],
                in_=src.rearrange("p (j r) -> p j r", r=world_size),
                axis=mybir.AxisListType.X,
                op=mybir.AluOpType.add,
            )

        MOVES = {0: ((1, 0), (1, 1)), 1: ((2, 0),), 2: ((2, 1),), 3: ((3, 0),), 4: ((3, 1),)}

        for i in range(RANGES):
            accs = []
            for t in range(RT):
                accs.append(bank([P, 512]))
            for g in range(G):
                for t in range(RT):
                    n0 = i * RW + t * P
                    nc.tensor.matmul_mx(
                        out=accs[t][:, 0:ROWS],
                        lhsT=w_tiles[(i, g)][:, t * P:(t + 1) * P].bitcast(FP8X4),
                        lhsT_scale=planes[4 * (g % 4):P, g // 4, n0:n0 + P],
                        rhs=x_codes[:, g, :].bitcast(FP8X4),
                        rhs_scale=x_plane[:, g, :],
                        start=(g == 0),
                        stop=(g == G - 1),
                    )
                if g == 1 and i >= 2 and i % 2 == 0:
                    emit_block(i // 2 - 1, nc.gpsimd)
            if i % 2 == 0:
                ot = opool.tile([P, 3, P], F32)
                o_t[i // 2] = ot
            evs = {}
            for t in range(1, RT, 2):
                ev = evp.tile([P, ROWS], F32)
                nc.scalar.copy(out=ev[:], in_=accs[t][:, 0:ROWS])
                evs[t] = ev
            for t in range(0, RT, 2):
                reduce_tile(i * RT + t, accs[t][:, 0:ROWS])
            for t in range(1, RT, 2):
                reduce_tile(i * RT + t, evs[t][:])
            for c, slot in MOVES.get(i, ()):
                move(c, slot)
            if i == 0:
                new_stage(3)
                stage(3, 0, nc.gpsimd, F32)
                stage(3, 1, nc.gpsimd, F32)
        emit_block(NT // BLK - 1, nc.sync)
